import numpy as np
import ml_dtypes


def mxq(x, axis, fmt="e4m3"):
    dtype, down = {"e4m3": (ml_dtypes.float8_e4m3fn, 7), "e5m2": (ml_dtypes.float8_e5m2, 14)}[fmt]
    v = np.moveaxis(np.asarray(x, np.float32).astype(ml_dtypes.bfloat16).astype(np.float64), axis, -1)
    blocks = v.reshape(v.shape[:-1] + (-1, 32))
    amax = np.abs(blocks).max(-1, keepdims=True)
    byte = np.maximum(np.where(amax > 0, np.frexp(amax)[1] - 1 + 127, 0) - down, 1)
    scale = np.exp2(byte - 127.0)
    codes = (blocks / scale).astype(np.float32).astype(dtype).astype(np.float64)
    return np.moveaxis((codes * scale).reshape(v.shape), -1, axis)


WIDE = False


def mx_kscale(k):
    if not WIDE:
        return np.ones(k)
    levels = np.array([10, -10, 5, -5, 0])
    if k % 512:
        return np.exp2(np.random.permutation(np.resize(levels, k // 32))).repeat(32)
    a = np.empty((k // 512, 16))
    for p in range(k // 512):
        a[p, :8] = np.random.permutation(np.resize(levels, 8))
        for g in range(8):
            far = levels[np.abs(levels - a[p, g]) >= 10]
            a[p, g + 8] = far[np.random.randint(len(far))]
    return np.exp2(a.ravel()).repeat(32)


BF16 = ml_dtypes.bfloat16


def bf(x):
    return np.asarray(x, np.float32).astype(BF16)


def f64(x):
    return np.asarray(x).astype(np.float64)


I, B, D, H, F = 1024, 4, 512, 4, 128
EPS = 1e-5


def setup_inputs():
    s = mx_kscale(D)
    return {"x": bf(np.random.standard_normal((I, B, D))),
            "gamma": bf((1.0 + 0.1 * np.random.standard_normal(D)) * s),
            "beta": bf(0.1 * np.random.standard_normal(D) * s),
            "Wq": bf(np.random.standard_normal((D, H * F)) * 1.5 / np.sqrt(D) / s[:, None]),
            "Wv": bf(np.random.standard_normal((D, H * F)) * 1.5 / np.sqrt(D) / s[:, None]),
            "u_bias": bf(np.random.standard_normal((H, F)) * 0.5),
            "v_bias": bf(np.random.standard_normal((H, F)) * 0.5)}


def reference(x, gamma, beta, Wq, Wv, u_bias, v_bias):
    x = f64(x)
    mu = x.mean(-1, keepdims=True)
    var = ((x - mu) ** 2).mean(-1, keepdims=True)
    h = (x - mu) / np.sqrt(var + EPS) * f64(gamma) + f64(beta)
    hq = mxq(h, 2, "e4m3")
    q = (hq @ mxq(f64(Wq), 0, "e4m3")).reshape(I, B, H, F)
    v = (hq @ mxq(f64(Wv), 0, "e4m3")).reshape(I, B, H, F)
    return q + f64(u_bias), q + f64(v_bias), q, v

@@ -1,0 +1,261 @@
+import concourse.mybir as mybir
+from concourse.masks import make_identity
+
+F32 = mybir.dt.float32
+BF16 = mybir.dt.bfloat16
+U32 = mybir.dt.uint32
+U8 = mybir.dt.uint8
+FP8X4 = mybir.dt.float8_e4m3fn_x4
+ACT = mybir.ActivationFunctionType
+ALU = mybir.AluOpType
+
+P = 128
+D = 512
+PACK = 4
+ROWS = 1024 * 4
+ROW_TILES = ROWS // P
+GROUP = 2
+GROUPS = ROW_TILES // GROUP
+BANK = 512
+CHUNKS_PER_BANK = BANK // (GROUP * P)
+LOAD_TILES = 4
+RUN = 4
+EPS = 1e-5
+
+FLOPS = 2 * ROWS * D * (2 * D)
+
+
+def tile_multiheadattentiowithrpe_pa_t_kernel(
+    tc, x, gamma, beta, Wq, Wv, u_bias, v_bias, out_0, out_1, out_2, out_3
+):
+    nc = tc.nc
+    x_rows = x.rearrange("(p a) b d -> p (a b) d", p=P)
+    out_rows = [
+        o.rearrange("(p a) b h f -> p (a b) (h f)", p=P) for o in (out_0, out_1, out_2, out_3)
+    ]
+
+    with (
+        tc.tile_pool(name="keep", bufs=1) as keep,
+        tc.tile_pool(name="small", bufs=4) as small,
+        tc.tile_pool(name="work", bufs=2) as work,
+        tc.tile_pool(name="stage", bufs=5) as stage,
+        tc.psum_pool(name="psum", bufs=2) as psum,
+        tc.manual_schedule(),
+    ):
+        x_home = {}
+
+        def load_rows(first, count):
+            chunk = keep.tile([P, count, D], BF16, name="x_sb%d" % first)
+            nc.sync.dma_start(out=chunk[:], in_=x_rows[:, first : first + count, :])
+            for i in range(count):
+                x_home[first + i] = (chunk, i)
+
+        def load_weight(weight, name):
+            raw = keep.tile([P, PACK, D], BF16, name=name)
+            nc.sync.dma_start(out=raw[:], in_=weight.rearrange("(p t) n -> p t n", t=PACK))
+            return raw
+
+        load_rows(0, GROUP)
+        load_rows(GROUP, GROUP)
+        wq_raw = load_weight(Wq, "wq_raw")
+        wv_raw = load_weight(Wv, "wv_raw")
+        for first in range(2 * GROUP, ROW_TILES, LOAD_TILES):
+            load_rows(first, LOAD_TILES)
+        w_raw = [wq_raw, wv_raw]
+
+        vec_rows = keep.tile([P, D], BF16, name="vec_rows")
+        nc.vector.memset(vec_rows[:], 0.0)
+        bias_row = keep.tile([P, 2, D], BF16, name="bias_row")
+        nc.vector.memset(bias_row[:], 0.0)
+        ones = keep.tile([P, P], BF16, name="ones")
+        nc.vector.memset(ones[:], 1.0)
+        minus_half = keep.tile([P, GROUP, 1], F32, name="minus_half")
+        nc.vector.memset(minus_half[:], -0.5)
+        nc.scalar.dma_start(out=vec_rows[0:1, :], in_=gamma.unsqueeze(0))
+        nc.scalar.dma_start(out=vec_rows[1:2, :], in_=beta.unsqueeze(0))
+        nc.scalar.dma_start(out=bias_row[0:1, 0, :], in_=u_bias.rearrange("h f -> (h f)").unsqueeze(0))
+        nc.scalar.dma_start(out=bias_row[0:1, 1, :], in_=v_bias.rearrange("h f -> (h f)").unsqueeze(0))
+        ident = keep.tile([P, P], F32, name="ident")
+        make_identity(nc, ident[:])
+        gain_offset = keep.tile([P, PACK, 2], F32, name="gain_offset")
+        biases = keep.tile([P, 2, D], F32, name="biases")
+        w_grouped = [
+            keep.tile([P, D, PACK], BF16, name="w_grouped%d" % w, align_bytes=64) for w in range(2)
+        ]
+        w_codes = keep.tile([P, 2, D], U32, name="w_codes", align_bytes=64)
+        w_scales = keep.tile([P, 2, D], U8, name="w_scales", align_bytes=64)
+
+        def turn_gamma_beta():
+            vec_rows_f32 = keep.tile([P, PACK, P], F32, name="vec_rows_f32")
+            nc.scalar.copy(out=vec_rows_f32[:], in_=vec_rows[:].rearrange("p (m t) -> p t m", t=PACK))
+            vec_cols = psum.tile([P, PACK, P], F32, tag="turned", name="vec_cols")
+            for t in range(PACK):
+                nc.tensor.transpose(vec_cols[:, t, :], vec_rows_f32[:, t, :], ident[:])
+            nc.scalar.copy(out=gain_offset[:], in_=vec_cols[:, :, 0:2])
+
+        def quantise_weights():
+            for w in range(2):
+                nc.vector.tensor_copy(
+                    out=w_grouped[w][:].rearrange("p (c i) t -> p c t i", i=RUN),
+                    in_=w_raw[w][:].rearrange("p t (c i) -> p c t i", i=RUN),
+                )
+            for w in range(2):
+                nc.vector.quantize_mx(
+                    out=w_codes[:, w, :].bitcast(FP8X4),
+                    scales=w_scales[:, w, :],
+                    in_=w_grouped[w][:].rearrange("p c t -> p (c t)"),
+                )
+
+        def spread_biases():
+            for b, tag in enumerate(("q_plain", "v_plain")):
+                bias_ps = psum.tile([P, D], F32, tag=tag, name="bias_ps")
+                nc.tensor.matmul(out=bias_ps[:], lhsT=ones[:], rhs=bias_row[:, b, :], start=True, stop=True)
+                nc.scalar.copy(out=biases[:, b, :], in_=bias_ps[:])
+
+        def rows_of(g):
+            homes = [x_home[g * GROUP + r] for r in range(GROUP)]
+            return [chunk[:, i, :] for chunk, i in homes]
+
+        live = {}
+
+        def row_statistics(g):
+            stats = small.tile([P, GROUP, 6], F32, tag="stats", name="stats")
+            for r, rows in enumerate(rows_of(g)):
+                nc.vector.bn_stats(out=stats[:, r, :], in_=rows)
+            live["stats", g] = stats
+
+        def mean_and_rstd(g):
+            mean_var = small.tile([P, GROUP, 2], F32, tag="mean_var", name="mean_var")
+            for r in range(GROUP):
+                nc.vector.bn_aggr(out=mean_var[:, r, :], in_=live["stats", g][:, r, :])
+            var_eps = small.tile([P, GROUP, 1], F32, tag="var_eps", name="var_eps")
+            nc.gpsimd.tensor_scalar(
+                out=var_eps[:], in0=mean_var[:, :, 1:2], scalar1=EPS, scalar2=None, op0=ALU.add
+            )
+            rstd = small.tile([P, GROUP, 1], F32, tag="rstd", name="rstd")
+            nc.gpsimd.tensor_tensor(out=rstd[:], in0=var_eps[:], in1=minus_half[:], op=ALU.pow)
+            mean_rstd = small.tile([P, GROUP, 1], F32, tag="mean_rstd", name="mean_rstd")
+            nc.gpsimd.tensor_tensor(out=mean_rstd[:], in0=mean_var[:, :, 0:1], in1=rstd[:], op=ALU.mult)
+            shift = small.tile([P, GROUP, 1], F32, tag="shift", name="shift")
+            nc.gpsimd.tensor_scalar(
+                out=shift[:], in0=mean_rstd[:], scalar1=-1.0, scalar2=0.0, op0=ALU.mult, op1=ALU.add
+            )
+            live["rstd", g] = rstd
+            live["shift", g] = shift
+
+        def normalise(g):
+            normal = work.tile([P, GROUP, D], F32, tag="normal", name="normal")
+            for r, rows in enumerate(rows_of(g)):
+                nc.scalar.activation(
+                    out=normal[:, r, :].rearrange("p (t m) -> p t m", t=PACK),
+                    in_=rows.rearrange("p (m t) -> p t m", t=PACK),
+                    func=ACT.Identity,
+                    scale=live["rstd", g][:, r, :], bias=live["shift", g][:, r, :],
+                )
+            live["normal", g] = normal
+
+        def turn(g):
+            banks = [
+                psum.tile([P, CHUNKS_PER_BANK, GROUP, P], F32, tag="turned", name="turned%d" % b)
+                for b in range(PACK // CHUNKS_PER_BANK)
+            ]
+            for r in range(GROUP):
+                for t in range(PACK):
+                    nc.tensor.transpose(
+                        banks[t // CHUNKS_PER_BANK][:, t % CHUNKS_PER_BANK, r, :],
+                        live["normal", g][:, r, t * P : (t + 1) * P],
+                        ident[:],
+                    )
+            live["turned", g] = banks
+
+        def scale_shift(g):
+            planes = work.tile([P, PACK, GROUP * P], BF16, tag="planes", name="planes")
+            for t in range(PACK):
+                bank = live["turned", g][t // CHUNKS_PER_BANK]
+                nc.scalar.activation(
+                    out=planes[:, t, :],
+                    in_=bank[:, t % CHUNKS_PER_BANK, :, :].rearrange("p r c -> p (r c)"),
+                    func=ACT.Identity,
+                    scale=gain_offset[:, t, 0:1],
+                    bias=gain_offset[:, t, 1:2],
+                )
+            live["planes", g] = planes
+
+        def quantise(g):
+            grouped = work.tile([P, GROUP * P, PACK], BF16, tag="grouped", name="grouped", align_bytes=64)
+            nc.vector.tensor_copy(
+                out=grouped[:].rearrange("p (c i) t -> p c t i", i=RUN),
+                in_=live["planes", g][:].rearrange("p t (c i) -> p c t i", i=RUN),
+            )
+            codes = work.tile([P, GROUP * P], U32, tag="codes", name="codes", align_bytes=64)
+            scales = work.tile([P, GROUP * P], U8, tag="scales", name="scales", align_bytes=64)
+            nc.vector.quantize_mx(
+                out=codes[:].bitcast(FP8X4),
+                scales=scales[:],
+                in_=grouped[:].rearrange("p c t -> p (c t)"),
+            )
+            live["codes", g] = codes
+            live["scales", g] = scales
+
+        def project(g):
+            for r in range(GROUP):
+                cols = slice(r * P, (r + 1) * P)
+                for tag, w in (("q_biased", 0), ("q_plain", 0), ("v_plain", 1)):
+                    acc = psum.tile([P, D], F32, tag=tag, name=tag)
+                    nc.tensor.matmul_mx(
+                        out=acc[:],
+                        lhsT=live["codes", g][:, cols].bitcast(FP8X4),
+                        lhsT_scale=live["scales", g][:, cols],
+                        rhs=w_codes[:, w, :].bitcast(FP8X4),
+                        rhs_scale=w_scales[:, w, :],
+                        start=True,
+                        stop=True,
+                    )
+                    live[tag, g, r] = acc
+
+        def finish(g, r):
+            if r == 0:
+                live["biased", g] = stage.tile([P, 2, GROUP, D], F32, tag="biased", name="biased")
+                live["plain", g] = stage.tile([P, 2, GROUP, D], F32, tag="plain", name="plain")
+            nc.vector.tensor_tensor(
+                out=live["biased", g][:, :, r, :],
+                in0=live["q_biased", g, r][:].unsqueeze(1).to_broadcast([P, 2, D]),
+                in1=biases[:],
+                op=ALU.add,
+            )
+            nc.scalar.copy(out=live["plain", g][:, 0, r, :], in_=live["q_plain", g, r][:])
+            nc.scalar.copy(out=live["plain", g][:, 1, r, :], in_=live["v_plain", g, r][:])
+
+        def store(g):
+            tiles = slice(g * GROUP, (g + 1) * GROUP)
+            nc.sync.dma_start(out=out_rows[0][:, tiles, :], in_=live["biased", g][:, 0, :, :])
+            nc.sync.dma_start(out=out_rows[1][:, tiles, :], in_=live["biased", g][:, 1, :, :])
+            nc.sync.dma_start(out=out_rows[2][:, tiles, :], in_=live["plain", g][:, 0, :, :])
+            nc.sync.dma_start(out=out_rows[3][:, tiles, :], in_=live["plain", g][:, 1, :, :])
+
+        turn_gamma_beta()
+        spread_biases()
+        for arriving in range(GROUPS + 4):
+            normalising = arriving - 1
+            turning = arriving - 2
+            packing = arriving - 3
+            leaving = arriving - 4
+            if 0 <= leaving:
+                project(leaving)
+            if 0 <= packing < GROUPS:
+                scale_shift(packing)
+            if 0 <= turning < GROUPS:
+                turn(turning)
+            if 0 <= leaving:
+                finish(leaving, 0)
+                finish(leaving, 1)
+                store(leaving)
+            if 0 <= normalising < GROUPS:
+                normalise(normalising)
+            if 0 <= packing < GROUPS:
+                quantise(packing)
+            if arriving < GROUPS:
+                row_statistics(arriving)
+                mean_and_rstd(arriving)
+            if arriving == 1:
+                quantise_weights()

@@ -15,10 +15,13 @@ PACK = 4
 ROWS = 1024 * 4
 ROW_TILES = ROWS // P
 GROUP = 2
-GROUPS = ROW_TILES // GROUP
+HEAD = 2
+TAIL = 2
+PAIRS = (ROW_TILES - HEAD - TAIL) // GROUP
+GROUPS = HEAD + PAIRS + TAIL
 BANK = 512
-CHUNKS_PER_BANK = BANK // (GROUP * P)
 LOAD_TILES = 4
+GPSIMD_EVERY = 2
 RUN = 4
 EPS = 1e-5
 
@@ -55,28 +58,31 @@ def tile_multiheadattentiowithrpe_pa_t_kernel(
             nc.sync.dma_start(out=raw[:], in_=weight.rearrange("(p t) n -> p t n", t=PACK))
             return raw
 
-        load_rows(0, GROUP)
-        load_rows(GROUP, GROUP)
+        load_rows(0, 1)
+        load_rows(1, 1)
         wq_raw = load_weight(Wq, "wq_raw")
         wv_raw = load_weight(Wv, "wv_raw")
-        for first in range(2 * GROUP, ROW_TILES, LOAD_TILES):
+        load_rows(2, 2)
+        for first in range(4, ROW_TILES, LOAD_TILES):
             load_rows(first, LOAD_TILES)
         w_raw = [wq_raw, wv_raw]
 
         vec_rows = keep.tile([P, D], BF16, name="vec_rows")
         nc.vector.memset(vec_rows[:], 0.0)
-        bias_row = keep.tile([P, 2, D], BF16, name="bias_row")
-        nc.vector.memset(bias_row[:], 0.0)
-        ones = keep.tile([P, P], BF16, name="ones")
-        nc.vector.memset(ones[:], 1.0)
         minus_half = keep.tile([P, GROUP, 1], F32, name="minus_half")
         nc.vector.memset(minus_half[:], -0.5)
+        minus_one = keep.tile([P, 1], F32, name="minus_one")
+        nc.vector.memset(minus_one[:], -1.0)
         nc.scalar.dma_start(out=vec_rows[0:1, :], in_=gamma.unsqueeze(0))
         nc.scalar.dma_start(out=vec_rows[1:2, :], in_=beta.unsqueeze(0))
-        nc.scalar.dma_start(out=bias_row[0:1, 0, :], in_=u_bias.rearrange("h f -> (h f)").unsqueeze(0))
-        nc.scalar.dma_start(out=bias_row[0:1, 1, :], in_=v_bias.rearrange("h f -> (h f)").unsqueeze(0))
+        nc.scalar.dma_start(out=vec_rows[2:3, :], in_=u_bias.rearrange("h f -> (h f)").unsqueeze(0))
+        nc.scalar.dma_start(out=vec_rows[3:4, :], in_=v_bias.rearrange("h f -> (h f)").unsqueeze(0))
         ident = keep.tile([P, P], F32, name="ident")
         make_identity(nc, ident[:])
+        ident_bf = keep.tile([P, P], BF16, name="ident_bf")
+        nc.vector.tensor_copy(out=ident_bf[:], in_=ident[:])
+        warm = keep.tile([P, 1], F32, name="warm")
+        nc.scalar.activation(out=warm[:], in_=minus_half[:, 0, :], func=ACT.Identity)
         gain_offset = keep.tile([P, PACK, 2], F32, name="gain_offset")
         biases = keep.tile([P, 2, D], F32, name="biases")
         w_grouped = [
@@ -86,121 +92,144 @@ def tile_multiheadattentiowithrpe_pa_t_kernel(
         w_scales = keep.tile([P, 2, D], U8, name="w_scales", align_bytes=64)
 
         def turn_gamma_beta():
-            vec_rows_f32 = keep.tile([P, PACK, P], F32, name="vec_rows_f32")
-            nc.scalar.copy(out=vec_rows_f32[:], in_=vec_rows[:].rearrange("p (m t) -> p t m", t=PACK))
-            vec_cols = psum.tile([P, PACK, P], F32, tag="turned", name="vec_cols")
+            vec_cols = psum.tile([P, PACK, P], BF16, tag="turned", name="vec_cols")
             for t in range(PACK):
-                nc.tensor.transpose(vec_cols[:, t, :], vec_rows_f32[:, t, :], ident[:])
+                nc.tensor.transpose(
+                    vec_cols[:, t, :], vec_rows[:].rearrange("p (m t) -> p t m", t=PACK)[:, t, :], ident_bf[:]
+                )
             nc.scalar.copy(out=gain_offset[:], in_=vec_cols[:, :, 0:2])
 
-        def quantise_weights():
-            for w in range(2):
-                nc.vector.tensor_copy(
-                    out=w_grouped[w][:].rearrange("p (c i) t -> p c t i", i=RUN),
-                    in_=w_raw[w][:].rearrange("p t (c i) -> p c t i", i=RUN),
-                )
-            for w in range(2):
-                nc.vector.quantize_mx(
-                    out=w_codes[:, w, :].bitcast(FP8X4),
-                    scales=w_scales[:, w, :],
-                    in_=w_grouped[w][:].rearrange("p c t -> p (c t)"),
-                )
+        def group_weight(w, copy, part=0, parts=1):
+            cols = slice(part * D // parts, (part + 1) * D // parts)
+            copy(
+                out=w_grouped[w][:, cols, :].rearrange("p (c i) t -> p c t i", i=RUN),
+                in_=w_raw[w][:, :, cols].rearrange("p t (c i) -> p c t i", i=RUN),
+            )
 
-        def spread_biases():
-            for b, tag in enumerate(("q_plain", "v_plain")):
-                bias_ps = psum.tile([P, D], F32, tag=tag, name="bias_ps")
-                nc.tensor.matmul(out=bias_ps[:], lhsT=ones[:], rhs=bias_row[:, b, :], start=True, stop=True)
-                nc.scalar.copy(out=biases[:, b, :], in_=bias_ps[:])
+        def quantise_weight(w):
+            nc.vector.quantize_mx(
+                out=w_codes[:, w, :].bitcast(FP8X4),
+                scales=w_scales[:, w, :],
+                in_=w_grouped[w][:].rearrange("p c t -> p (c t)"),
+            )
+
+        def spread_bias(b):
+            bias_ps = psum.tile([P, D], F32, tag=("q_plain", "v_plain")[b], name="bias_ps")
+            nc.tensor.matmul(
+                out=bias_ps[:], lhsT=ident_bf[:, 2 + b : 3 + b].to_broadcast([P, P]), rhs=vec_rows[:],
+                start=True, stop=True,
+            )
+            nc.scalar.copy(out=biases[:, b, :], in_=bias_ps[:])
+
+        def tiles_of(g):
+            if g < HEAD:
+                return g, 1
+            if g < HEAD + PAIRS:
+                return HEAD + (g - HEAD) * GROUP, GROUP
+            return ROW_TILES - GROUPS + g, 1
 
         def rows_of(g):
-            homes = [x_home[g * GROUP + r] for r in range(GROUP)]
+            first, count = tiles_of(g)
+            homes = [x_home[first + r] for r in range(count)]
             return [chunk[:, i, :] for chunk, i in homes]
 
         live = {}
 
-        def row_statistics(g):
-            stats = small.tile([P, GROUP, 6], F32, tag="stats", name="stats")
-            for r, rows in enumerate(rows_of(g)):
-                nc.vector.bn_stats(out=stats[:, r, :], in_=rows)
-            live["stats", g] = stats
+        def row_statistics(g, r):
+            if r == 0:
+                live["stats", g] = small.tile([P, GROUP, 6], F32, tag="stats", name="stats")
+            nc.vector.bn_stats(out=live["stats", g][:, r, :], in_=rows_of(g)[r])
 
         def mean_and_rstd(g):
             mean_var = small.tile([P, GROUP, 2], F32, tag="mean_var", name="mean_var")
-            for r in range(GROUP):
+            count = tiles_of(g)[1]
+            for r in range(count):
                 nc.vector.bn_aggr(out=mean_var[:, r, :], in_=live["stats", g][:, r, :])
             var_eps = small.tile([P, GROUP, 1], F32, tag="var_eps", name="var_eps")
             nc.gpsimd.tensor_scalar(
-                out=var_eps[:], in0=mean_var[:, :, 1:2], scalar1=EPS, scalar2=None, op0=ALU.add
+                out=var_eps[:, :count], in0=mean_var[:, :count, 1:2], scalar1=EPS, scalar2=None, op0=ALU.add
             )
             rstd = small.tile([P, GROUP, 1], F32, tag="rstd", name="rstd")
-            nc.gpsimd.tensor_tensor(out=rstd[:], in0=var_eps[:], in1=minus_half[:], op=ALU.pow)
-            mean_rstd = small.tile([P, GROUP, 1], F32, tag="mean_rstd", name="mean_rstd")
-            nc.gpsimd.tensor_tensor(out=mean_rstd[:], in0=mean_var[:, :, 0:1], in1=rstd[:], op=ALU.mult)
-            shift = small.tile([P, GROUP, 1], F32, tag="shift", name="shift")
-            nc.gpsimd.tensor_scalar(
-                out=shift[:], in0=mean_rstd[:], scalar1=-1.0, scalar2=0.0, op0=ALU.mult, op1=ALU.add
+            nc.gpsimd.tensor_tensor(
+                out=rstd[:, :count], in0=var_eps[:, :count], in1=minus_half[:, :count], op=ALU.pow
             )
+            shift = small.tile([P, GROUP, 1], F32, tag="shift", name="shift")
+            for r in range(count):
+                nc.gpsimd.tensor_scalar(
+                    out=shift[:, r, :], in0=mean_var[:, r, 0:1], scalar1=rstd[:, r, :], scalar2=minus_one[:],
+                    op0=ALU.mult, op1=ALU.mult,
+                )
             live["rstd", g] = rstd
             live["shift", g] = shift
 
         def normalise(g):
             normal = work.tile([P, GROUP, D], F32, tag="normal", name="normal")
             for r, rows in enumerate(rows_of(g)):
-                nc.scalar.activation(
-                    out=normal[:, r, :].rearrange("p (t m) -> p t m", t=PACK),
-                    in_=rows.rearrange("p (m t) -> p t m", t=PACK),
-                    func=ACT.Identity,
-                    scale=live["rstd", g][:, r, :], bias=live["shift", g][:, r, :],
-                )
+                by_m = rows.rearrange("p (m t) -> p t m", t=PACK)
+                by_t = normal[:, r, :].rearrange("p (t m) -> p t m", t=PACK)
+                rstd = live["rstd", g][:, r, :]
+                shift = live["shift", g][:, r, :]
+                if r == 1 and g % GPSIMD_EVERY == 0:
+                    nc.gpsimd.tensor_scalar(
+                        out=by_t, in0=by_m, scalar1=rstd, scalar2=shift, op0=ALU.mult, op1=ALU.add
+                    )
+                else:
+                    nc.scalar.activation(out=by_t, in_=by_m, func=ACT.Identity, scale=rstd, bias=shift)
             live["normal", g] = normal
 
         def turn(g):
+            count = tiles_of(g)[1]
+            per_bank = BANK // (count * P)
             banks = [
-                psum.tile([P, CHUNKS_PER_BANK, GROUP, P], F32, tag="turned", name="turned%d" % b)
-                for b in range(PACK // CHUNKS_PER_BANK)
+                psum.tile([P, per_bank, count, P], F32, tag="turned", name="turned%d" % b)
+                for b in range(PACK // per_bank)
             ]
-            for r in range(GROUP):
+            chunks = [banks[t // per_bank][:, t % per_bank, :, :] for t in range(PACK)]
+            for r in range(count):
                 for t in range(PACK):
                     nc.tensor.transpose(
-                        banks[t // CHUNKS_PER_BANK][:, t % CHUNKS_PER_BANK, r, :],
-                        live["normal", g][:, r, t * P : (t + 1) * P],
-                        ident[:],
+                        chunks[t][:, r, :], live["normal", g][:, r, t * P : (t + 1) * P], ident[:]
                     )
-            live["turned", g] = banks
+            live["turned", g] = chunks
 
         def scale_shift(g):
-            planes = work.tile([P, PACK, GROUP * P], BF16, tag="planes", name="planes")
+            columns = tiles_of(g)[1] * P
+            planes = work.tile([P, PACK, columns], BF16, tag="planes", name="planes")
             for t in range(PACK):
-                bank = live["turned", g][t // CHUNKS_PER_BANK]
                 nc.scalar.activation(
                     out=planes[:, t, :],
-                    in_=bank[:, t % CHUNKS_PER_BANK, :, :].rearrange("p r c -> p (r c)"),
+                    in_=live["turned", g][t].rearrange("p r c -> p (r c)"),
                     func=ACT.Identity,
                     scale=gain_offset[:, t, 0:1],
                     bias=gain_offset[:, t, 1:2],
                 )
             live["planes", g] = planes
 
-        def quantise(g):
-            grouped = work.tile([P, GROUP * P, PACK], BF16, tag="grouped", name="grouped", align_bytes=64)
+        def pack(g):
+            columns = tiles_of(g)[1] * P
+            grouped = work.tile([P, columns, PACK], BF16, tag="grouped", name="grouped", align_bytes=64)
             nc.vector.tensor_copy(
                 out=grouped[:].rearrange("p (c i) t -> p c t i", i=RUN),
                 in_=live["planes", g][:].rearrange("p t (c i) -> p c t i", i=RUN),
             )
-            codes = work.tile([P, GROUP * P], U32, tag="codes", name="codes", align_bytes=64)
-            scales = work.tile([P, GROUP * P], U8, tag="scales", name="scales", align_bytes=64)
+            live["grouped", g] = grouped
+
+        def quantise(g):
+            columns = tiles_of(g)[1] * P
+            codes = work.tile([P, columns], U32, tag="codes", name="codes", align_bytes=64)
+            scales = work.tile([P, columns], U8, tag="scales", name="scales", align_bytes=64)
             nc.vector.quantize_mx(
                 out=codes[:].bitcast(FP8X4),
                 scales=scales[:],
-                in_=grouped[:].rearrange("p c t -> p (c t)"),
+                in_=live["grouped", g][:].rearrange("p c t -> p (c t)"),
             )
             live["codes", g] = codes
             live["scales", g] = scales
 
-        def project(g):
-            for r in range(GROUP):
+        def project(g, wanted):
+            for r in range(tiles_of(g)[1]):
                 cols = slice(r * P, (r + 1) * P)
-                for tag, w in (("q_biased", 0), ("q_plain", 0), ("v_plain", 1)):
+                for tag, w in wanted:
                     acc = psum.tile([P, D], F32, tag=tag, name=tag)
                     nc.tensor.matmul_mx(
                         out=acc[:],
@@ -213,49 +242,86 @@ def tile_multiheadattentiowithrpe_pa_t_kernel(
                     )
                     live[tag, g, r] = acc
 
-        def finish(g, r):
-            if r == 0:
-                live["biased", g] = stage.tile([P, 2, GROUP, D], F32, tag="biased", name="biased")
-                live["plain", g] = stage.tile([P, 2, GROUP, D], F32, tag="plain", name="plain")
+        Q_PASSES = (("q_biased", 0), ("q_plain", 0))
+        V_PASSES = (("v_plain", 1),)
+
+        def open_stage(g):
+            count = tiles_of(g)[1]
+            live["biased", g] = stage.tile([P, 2, count, D], F32, tag="biased", name="biased")
+            live["plain", g] = stage.tile([P, 2, count, D], F32, tag="plain", name="plain")
+
+        def add_biases(g, r):
             nc.vector.tensor_tensor(
                 out=live["biased", g][:, :, r, :],
                 in0=live["q_biased", g, r][:].unsqueeze(1).to_broadcast([P, 2, D]),
                 in1=biases[:],
                 op=ALU.add,
             )
-            nc.scalar.copy(out=live["plain", g][:, 0, r, :], in_=live["q_plain", g, r][:])
-            nc.scalar.copy(out=live["plain", g][:, 1, r, :], in_=live["v_plain", g, r][:])
 
-        def store(g):
-            tiles = slice(g * GROUP, (g + 1) * GROUP)
-            nc.sync.dma_start(out=out_rows[0][:, tiles, :], in_=live["biased", g][:, 0, :, :])
-            nc.sync.dma_start(out=out_rows[1][:, tiles, :], in_=live["biased", g][:, 1, :, :])
-            nc.sync.dma_start(out=out_rows[2][:, tiles, :], in_=live["plain", g][:, 0, :, :])
-            nc.sync.dma_start(out=out_rows[3][:, tiles, :], in_=live["plain", g][:, 1, :, :])
+        def copy_out(g, r, place):
+            tag = ("q_plain", "v_plain")[place]
+            nc.scalar.copy(out=live["plain", g][:, place, r, :], in_=live[tag, g, r][:])
 
-        turn_gamma_beta()
-        spread_biases()
-        for arriving in range(GROUPS + 4):
-            normalising = arriving - 1
-            turning = arriving - 2
-            packing = arriving - 3
-            leaving = arriving - 4
-            if 0 <= leaving:
-                project(leaving)
-            if 0 <= packing < GROUPS:
-                scale_shift(packing)
-            if 0 <= turning < GROUPS:
-                turn(turning)
-            if 0 <= leaving:
-                finish(leaving, 0)
-                finish(leaving, 1)
-                store(leaving)
-            if 0 <= normalising < GROUPS:
-                normalise(normalising)
-            if 0 <= packing < GROUPS:
-                quantise(packing)
-            if arriving < GROUPS:
-                row_statistics(arriving)
-                mean_and_rstd(arriving)
-            if arriving == 1:
-                quantise_weights()
+        def finish(g, r):
+            add_biases(g, r)
+            copy_out(g, r, 0)
+            copy_out(g, r, 1)
+
+        def store(g, r, count):
+            first = tiles_of(g)[0] + r
+            tiles = slice(first, first + count)
+            part = slice(r, r + count)
+            nc.sync.dma_start(out=out_rows[0][:, tiles, :], in_=live["biased", g][:, 0, part, :])
+            nc.sync.dma_start(out=out_rows[1][:, tiles, :], in_=live["biased", g][:, 1, part, :])
+            nc.sync.dma_start(out=out_rows[2][:, tiles, :], in_=live["plain", g][:, 0, part, :])
+            nc.sync.dma_start(out=out_rows[3][:, tiles, :], in_=live["plain", g][:, 1, part, :])
+
+        for a in range(GROUPS + 3):
+            if a == 0:
+                turn_gamma_beta()
+            if 0 <= a - 0 < GROUPS:
+                row_statistics(a - 0, 0)
+            if 0 <= a - 0 < GROUPS:
+                if tiles_of(a - 0)[1] > 1:
+                    row_statistics(a - 0, 1)
+            if 0 <= a - 2 < GROUPS:
+                scale_shift(a - 2)
+            if 0 <= a - 1 < GROUPS:
+                normalise(a - 1)
+            if 0 <= a - 1 < GROUPS:
+                turn(a - 1)
+            if 0 <= a - 3 < GROUPS:
+                open_stage(a - 3)
+                add_biases(a - 3, 0)
+            if 0 <= a - 3 < GROUPS:
+                copy_out(a - 3, 0, 0)
+                copy_out(a - 3, 0, 1)
+            if 0 <= a - 0 < GROUPS:
+                mean_and_rstd(a - 0)
+            if 0 <= a - 2 < GROUPS:
+                pack(a - 2)
+            if 0 <= a - 3 < GROUPS:
+                if tiles_of(a - 3)[1] > 1:
+                    add_biases(a - 3, 1)
+            if 0 <= a - 3 < GROUPS:
+                if tiles_of(a - 3)[1] > 1:
+                    copy_out(a - 3, 1, 0)
+                    copy_out(a - 3, 1, 1)
+            if a == 0:
+                group_weight(0, nc.vector.tensor_copy)
+            if a == 1:
+                group_weight(1, nc.scalar.copy)
+            if a == 1:
+                spread_bias(0)
+            if a == 1:
+                quantise_weight(0)
+            if a == 2:
+                spread_bias(1)
+            if 0 <= a - 2 < GROUPS:
+                quantise(a - 2)
+            if a == 2:
+                quantise_weight(1)
+            if 0 <= a - 2 < GROUPS:
+                project(a - 2, Q_PASSES + V_PASSES)
+            if 0 <= a - 3 < GROUPS:
+                store(a - 3, 0, tiles_of(a - 3)[1])

@@ -16,7 +16,10 @@ ROWS = 1024 * 4
 ROW_TILES = ROWS // P
 GROUP = 2
 HEAD = 2
-TAIL = 2
+SINGLE_BLOCKS = 8
+PAIR_BLOCKS = 10
+LONG_BLOCK = 4
+TAIL = 0
 PAIRS = (ROW_TILES - HEAD - TAIL) // GROUP
 GROUPS = HEAD + PAIRS + TAIL
 BANK = 512
@@ -41,7 +44,7 @@ def tile_multiheadattentiowithrpe_pa_t_kernel(
         tc.tile_pool(name="keep", bufs=1) as keep,
         tc.tile_pool(name="small", bufs=4) as small,
         tc.tile_pool(name="work", bufs=2) as work,
-        tc.tile_pool(name="stage", bufs=5) as stage,
+        tc.tile_pool(name="stage", bufs=4) as stage,
         tc.psum_pool(name="psum", bufs=2) as psum,
         tc.manual_schedule(),
     ):
@@ -60,9 +63,9 @@ def tile_multiheadattentiowithrpe_pa_t_kernel(
 
         load_rows(0, 1)
         load_rows(1, 1)
+        load_rows(2, 2)
         wq_raw = load_weight(Wq, "wq_raw")
         wv_raw = load_weight(Wv, "wv_raw")
-        load_rows(2, 2)
         for first in range(4, ROW_TILES, LOAD_TILES):
             load_rows(first, LOAD_TILES)
         w_raw = [wq_raw, wv_raw]
@@ -71,6 +74,9 @@ def tile_multiheadattentiowithrpe_pa_t_kernel(
         nc.vector.memset(vec_rows[:], 0.0)
         minus_half = keep.tile([P, GROUP, 1], F32, name="minus_half")
         nc.vector.memset(minus_half[:], -0.5)
+        stats = keep.tile([P, ROW_TILES, 9], F32, name="stats")
+        nc.gpsimd.memset(stats[:, :, 6:8], 0.0)
+        nc.gpsimd.memset(stats[:, :, 8:9], D * EPS)
         minus_one = keep.tile([P, 1], F32, name="minus_one")
         nc.vector.memset(minus_one[:], -1.0)
         nc.scalar.dma_start(out=vec_rows[0:1, :], in_=gamma.unsqueeze(0))
@@ -97,7 +103,10 @@ def tile_multiheadattentiowithrpe_pa_t_kernel(
                 nc.tensor.transpose(
                     vec_cols[:, t, :], vec_rows[:].rearrange("p (m t) -> p t m", t=PACK)[:, t, :], ident_bf[:]
                 )
-            nc.scalar.copy(out=gain_offset[:], in_=vec_cols[:, :, 0:2])
+            live["vec_cols"] = vec_cols
+
+        def take_gain():
+            nc.scalar.copy(out=gain_offset[:], in_=live["vec_cols"][:, :, 0:2])
 
         def group_weight(w, copy, part=0, parts=1):
             cols = slice(part * D // parts, (part + 1) * D // parts)
@@ -136,30 +145,32 @@ def tile_multiheadattentiowithrpe_pa_t_kernel(
         live = {}
 
         def row_statistics(g, r):
-            if r == 0:
-                live["stats", g] = small.tile([P, GROUP, 6], F32, tag="stats", name="stats")
-            nc.vector.bn_stats(out=live["stats", g][:, r, :], in_=rows_of(g)[r])
+            nc.vector.bn_stats(out=stats[:, tiles_of(g)[0] + r, 0:6], in_=rows_of(g)[r])
+
+        def norm_engine(g, r):
+            return "V" if g < HEAD or r == 1 else "S"
 
         def mean_and_rstd(g):
+            first, count = tiles_of(g)
             mean_var = small.tile([P, GROUP, 2], F32, tag="mean_var", name="mean_var")
-            count = tiles_of(g)[1]
             for r in range(count):
-                nc.vector.bn_aggr(out=mean_var[:, r, :], in_=live["stats", g][:, r, :])
-            var_eps = small.tile([P, GROUP, 1], F32, tag="var_eps", name="var_eps")
-            nc.gpsimd.tensor_scalar(
-                out=var_eps[:, :count], in0=mean_var[:, :count, 1:2], scalar1=EPS, scalar2=None, op0=ALU.add
-            )
+                nc.vector.bn_aggr(out=mean_var[:, r, :], in_=stats[:, first + r, :])
             rstd = small.tile([P, GROUP, 1], F32, tag="rstd", name="rstd")
             nc.gpsimd.tensor_tensor(
-                out=rstd[:, :count], in0=var_eps[:, :count], in1=minus_half[:, :count], op=ALU.pow
+                out=rstd[:, :count], in0=mean_var[:, :count, 1:2], in1=minus_half[:, :count], op=ALU.pow
             )
+            live["mean_var", g] = mean_var
+            live["rstd", g] = rstd
+            if all(norm_engine(g, r) == "V" for r in range(count)):
+                return
             shift = small.tile([P, GROUP, 1], F32, tag="shift", name="shift")
             for r in range(count):
+                if norm_engine(g, r) == "V":
+                    continue
                 nc.gpsimd.tensor_scalar(
                     out=shift[:, r, :], in0=mean_var[:, r, 0:1], scalar1=rstd[:, r, :], scalar2=minus_one[:],
                     op0=ALU.mult, op1=ALU.mult,
                 )
-            live["rstd", g] = rstd
             live["shift", g] = shift
 
         def normalise(g):
@@ -168,8 +179,14 @@ def tile_multiheadattentiowithrpe_pa_t_kernel(
                 by_m = rows.rearrange("p (m t) -> p t m", t=PACK)
                 by_t = normal[:, r, :].rearrange("p (t m) -> p t m", t=PACK)
                 rstd = live["rstd", g][:, r, :]
+                if norm_engine(g, r) == "V":
+                    nc.vector.tensor_scalar(
+                        out=by_t, in0=by_m, scalar1=live["mean_var", g][:, r, 0:1], scalar2=rstd,
+                        op0=ALU.subtract, op1=ALU.mult,
+                    )
+                    continue
                 shift = live["shift", g][:, r, :]
-                if r == 1 and g % GPSIMD_EVERY == 0:
+                if norm_engine(g, r) == "G":
                     nc.gpsimd.tensor_scalar(
                         out=by_t, in0=by_m, scalar1=rstd, scalar2=shift, op0=ALU.mult, op1=ALU.add
                     )
@@ -205,13 +222,20 @@ def tile_multiheadattentiowithrpe_pa_t_kernel(
                 )
             live["planes", g] = planes
 
+        def pack_on_gpsimd(g):
+            return g > HEAD
+
         def pack(g):
             columns = tiles_of(g)[1] * P
             grouped = work.tile([P, columns, PACK], BF16, tag="grouped", name="grouped", align_bytes=64)
-            nc.vector.tensor_copy(
-                out=grouped[:].rearrange("p (c i) t -> p c t i", i=RUN),
-                in_=live["planes", g][:].rearrange("p t (c i) -> p c t i", i=RUN),
-            )
+            by_row = grouped[:].rearrange("p (c i) t -> p c t i", i=RUN)
+            by_plane = live["planes", g][:].rearrange("p t (c i) -> p c t i", i=RUN)
+            if pack_on_gpsimd(g):
+                nc.gpsimd.tensor_scalar(
+                    out=by_row, in0=by_plane, scalar1=1.0, scalar2=0.0, op0=ALU.mult, op1=ALU.add
+                )
+            else:
+                nc.vector.tensor_copy(out=by_row, in_=by_plane)
             live["grouped", g] = grouped
 
         def quantise(g):
@@ -245,83 +269,126 @@ def tile_multiheadattentiowithrpe_pa_t_kernel(
         Q_PASSES = (("q_biased", 0), ("q_plain", 0))
         V_PASSES = (("v_plain", 1),)
 
-        def open_stage(g):
-            count = tiles_of(g)[1]
-            live["biased", g] = stage.tile([P, 2, count, D], F32, tag="biased", name="biased")
-            live["plain", g] = stage.tile([P, 2, count, D], F32, tag="plain", name="plain")
+        blocks = [1] * SINGLE_BLOCKS + [GROUP] * PAIR_BLOCKS
+        while sum(blocks) < ROW_TILES:
+            blocks.append(min(LONG_BLOCK, ROW_TILES - sum(blocks)))
+        block_of = [(sum(blocks[:b]), count) for b, count in enumerate(blocks) for i in range(count)]
+
+        def open_stage(i):
+            first, count = block_of[i]
+            if ("biased", i) in live:
+                return
+            if i == first:
+                live["biased"] = stage.tile([P, 2, count, D], F32, tag="biased", name="biased")
+                live["plain"] = stage.tile([P, 2, count, D], F32, tag="plain", name="plain")
+            live["biased", i] = live["biased"]
+            live["plain", i] = live["plain"]
 
         def add_biases(g, r):
+            i = tiles_of(g)[0] + r
+            open_stage(i)
             nc.vector.tensor_tensor(
-                out=live["biased", g][:, :, r, :],
+                out=live["biased", i][:, :, i - block_of[i][0], :],
                 in0=live["q_biased", g, r][:].unsqueeze(1).to_broadcast([P, 2, D]),
                 in1=biases[:],
                 op=ALU.add,
             )
 
-        def copy_out(g, r, place):
-            tag = ("q_plain", "v_plain")[place]
-            nc.scalar.copy(out=live["plain", g][:, place, r, :], in_=live[tag, g, r][:])
+        def copy_out(g, r, wanted=(0, 1)):
+            i = tiles_of(g)[0] + r
+            open_stage(i)
+            for place in wanted:
+                acc = live[("q_plain", "v_plain")[place], g, r]
+                nc.scalar.copy(out=live["plain", i][:, place, i - block_of[i][0], :], in_=acc[:])
 
-        def finish(g, r):
-            add_biases(g, r)
-            copy_out(g, r, 0)
-            copy_out(g, r, 1)
+        def store(g, r):
+            first, count = block_of[tiles_of(g)[0] + r]
+            if tiles_of(g)[0] + r == first + count - 1:
+                tiles = slice(first, first + count)
+                nc.sync.dma_start(out=out_rows[0][:, tiles, :], in_=live["biased", first][:, 0, :, :])
+                nc.sync.dma_start(out=out_rows[1][:, tiles, :], in_=live["biased", first][:, 1, :, :])
+                nc.sync.dma_start(out=out_rows[2][:, tiles, :], in_=live["plain", first][:, 0, :, :])
+                nc.sync.dma_start(out=out_rows[3][:, tiles, :], in_=live["plain", first][:, 1, :, :])
 
-        def store(g, r, count):
-            first = tiles_of(g)[0] + r
-            tiles = slice(first, first + count)
-            part = slice(r, r + count)
-            nc.sync.dma_start(out=out_rows[0][:, tiles, :], in_=live["biased", g][:, 0, part, :])
-            nc.sync.dma_start(out=out_rows[1][:, tiles, :], in_=live["biased", g][:, 1, part, :])
-            nc.sync.dma_start(out=out_rows[2][:, tiles, :], in_=live["plain", g][:, 0, part, :])
-            nc.sync.dma_start(out=out_rows[3][:, tiles, :], in_=live["plain", g][:, 1, part, :])
-
-        for a in range(GROUPS + 3):
-            if a == 0:
-                turn_gamma_beta()
-            if 0 <= a - 0 < GROUPS:
-                row_statistics(a - 0, 0)
-            if 0 <= a - 0 < GROUPS:
-                if tiles_of(a - 0)[1] > 1:
-                    row_statistics(a - 0, 1)
-            if 0 <= a - 2 < GROUPS:
+        row_statistics(0, 0)
+        mean_and_rstd(0)
+        row_statistics(1, 0)
+        mean_and_rstd(1)
+        turn_gamma_beta()
+        take_gain()
+        spread_bias(0)
+        spread_bias(1)
+        normalise(0)
+        turn(0)
+        row_statistics(2, 0)
+        row_statistics(2, 1)
+        group_weight(0, nc.vector.tensor_copy)
+        scale_shift(0)
+        mean_and_rstd(2)
+        normalise(1)
+        turn(1)
+        quantise_weight(0)
+        pack(0)
+        group_weight(1, nc.scalar.copy, 0, 2)
+        scale_shift(1)
+        row_statistics(3, 0)
+        quantise(0)
+        project(0, Q_PASSES)
+        pack(1)
+        row_statistics(3, 1)
+        normalise(2)
+        turn(2)
+        group_weight(1, nc.scalar.copy, 1, 2)
+        quantise(1)
+        project(1, Q_PASSES)
+        mean_and_rstd(3)
+        add_biases(0, 0)
+        copy_out(0, 0, (0,))
+        scale_shift(2)
+        quantise_weight(1)
+        add_biases(1, 0)
+        copy_out(1, 0, (0,))
+        project(0, V_PASSES)
+        project(1, V_PASSES)
+        pack(2)
+        row_statistics(4, 0)
+        normalise(3)
+        turn(3)
+        copy_out(0, 0, (1,))
+        store(0, 0)
+        copy_out(1, 0, (1,))
+        store(1, 0)
+        row_statistics(4, 1)
+        mean_and_rstd(4)
+        for a in range(5, GROUPS + 3):
+            if a - 3 < GROUPS:
+                quantise(a - 3)
+            if a - 3 < GROUPS:
+                project(a - 3, Q_PASSES + V_PASSES)
+            if a - 2 < GROUPS:
                 scale_shift(a - 2)
-            if 0 <= a - 1 < GROUPS:
-                normalise(a - 1)
-            if 0 <= a - 1 < GROUPS:
-                turn(a - 1)
-            if 0 <= a - 3 < GROUPS:
-                open_stage(a - 3)
-                add_biases(a - 3, 0)
-            if 0 <= a - 3 < GROUPS:
-                copy_out(a - 3, 0, 0)
-                copy_out(a - 3, 0, 1)
-            if 0 <= a - 0 < GROUPS:
-                mean_and_rstd(a - 0)
-            if 0 <= a - 2 < GROUPS:
+            if a - 2 < GROUPS:
                 pack(a - 2)
-            if 0 <= a - 3 < GROUPS:
+            if a < GROUPS:
+                row_statistics(a, 0)
+            if a - 3 < GROUPS:
+                add_biases(a - 3, 0)
+            if a < GROUPS:
+                if tiles_of(a)[1] > 1:
+                    row_statistics(a, 1)
+            if a - 1 < GROUPS:
+                normalise(a - 1)
+            if a - 1 < GROUPS:
+                turn(a - 1)
+            if a < GROUPS:
+                mean_and_rstd(a)
+            if a - 3 < GROUPS:
+                copy_out(a - 3, 0)
+                store(a - 3, 0)
+            if a - 3 < GROUPS:
                 if tiles_of(a - 3)[1] > 1:
                     add_biases(a - 3, 1)
-            if 0 <= a - 3 < GROUPS:
+            if a - 3 < GROUPS:
                 if tiles_of(a - 3)[1] > 1:
-                    copy_out(a - 3, 1, 0)
-                    copy_out(a - 3, 1, 1)
-            if a == 0:
-                group_weight(0, nc.vector.tensor_copy)
-            if a == 1:
-                group_weight(1, nc.scalar.copy)
-            if a == 1:
-                spread_bias(0)
-            if a == 1:
-                quantise_weight(0)
-            if a == 2:
-                spread_bias(1)
-            if 0 <= a - 2 < GROUPS:
-                quantise(a - 2)
-            if a == 2:
-                quantise_weight(1)
-            if 0 <= a - 2 < GROUPS:
-                project(a - 2, Q_PASSES + V_PASSES)
-            if 0 <= a - 3 < GROUPS:
-                store(a - 3, 0, tiles_of(a - 3)[1])
+                    copy_out(a - 3, 1)
+                    store(a - 3, 1)

@@ -16,9 +16,8 @@ ROWS = 1024 * 4
 ROW_TILES = ROWS // P
 GROUP = 2
 HEAD = 2
-SINGLE_BLOCKS = 8
-PAIR_BLOCKS = 10
-LONG_BLOCK = 4
+SINGLES_BIASED = 8
+SINGLES_PLAIN = 8
 TAIL = 0
 PAIRS = (ROW_TILES - HEAD - TAIL) // GROUP
 GROUPS = HEAD + PAIRS + TAIL
@@ -35,9 +34,9 @@ def tile_multiheadattentiowithrpe_pa_t_kernel(
     tc, x, gamma, beta, Wq, Wv, u_bias, v_bias, out_0, out_1, out_2, out_3
 ):
     nc = tc.nc
-    x_rows = x.rearrange("(p a) b d -> p (a b) d", p=P)
+    x_rows = x.rearrange("(j i) (c r) d -> (i c) j r d", i=P // 2, c=2)
     out_rows = [
-        o.rearrange("(p a) b h f -> p (a b) (h f)", p=P) for o in (out_0, out_1, out_2, out_3)
+        o.rearrange("(j i) (c r) h f -> (i c) j r (h f)", i=P // 2, c=2) for o in (out_0, out_1, out_2, out_3)
     ]
 
     with (
@@ -52,7 +51,14 @@ def tile_multiheadattentiowithrpe_pa_t_kernel(
 
         def load_rows(first, count):
             chunk = keep.tile([P, count, D], BF16, name="x_sb%d" % first)
-            nc.sync.dma_start(out=chunk[:], in_=x_rows[:, first : first + count, :])
+            pair = first // GROUP
+            if count == 1:
+                nc.sync.dma_start(out=chunk[:, 0, :], in_=x_rows[:, pair, first % GROUP, :])
+            else:
+                nc.sync.dma_start(
+                    out=chunk[:].rearrange("p (j r) d -> p j r d", r=GROUP),
+                    in_=x_rows[:, pair : pair + count // GROUP, :, :],
+                )
             for i in range(count):
                 x_home[first + i] = (chunk, i)
 
@@ -114,6 +120,9 @@ def tile_multiheadattentiowithrpe_pa_t_kernel(
                 out=w_grouped[w][:, cols, :].rearrange("p (c i) t -> p c t i", i=RUN),
                 in_=w_raw[w][:, :, cols].rearrange("p t (c i) -> p c t i", i=RUN),
             )
+
+        def gp_copy(out, in_):
+            nc.gpsimd.tensor_scalar(out=out, in0=in_, scalar1=1.0, scalar2=0.0, op0=ALU.mult, op1=ALU.add)
 
         def quantise_weight(w):
             nc.vector.quantize_mx(
@@ -269,46 +278,53 @@ def tile_multiheadattentiowithrpe_pa_t_kernel(
         Q_PASSES = (("q_biased", 0), ("q_plain", 0))
         V_PASSES = (("v_plain", 1),)
 
-        blocks = [1] * SINGLE_BLOCKS + [GROUP] * PAIR_BLOCKS
-        while sum(blocks) < ROW_TILES:
-            blocks.append(min(LONG_BLOCK, ROW_TILES - sum(blocks)))
-        block_of = [(sum(blocks[:b]), count) for b, count in enumerate(blocks) for i in range(count)]
+        block_of = {}
+        for kind, singles in (("biased", SINGLES_BIASED), ("plain", SINGLES_PLAIN)):
+            first = 0
+            lengths = [1] * singles + [GROUP] * ROW_TILES
+            while first < ROW_TILES:
+                count = min(lengths.pop(0), ROW_TILES - first)
+                for i in range(first, first + count):
+                    block_of[kind, i] = (first, count)
+                first += count
 
-        def open_stage(i):
-            first, count = block_of[i]
-            if ("biased", i) in live:
-                return
-            if i == first:
-                live["biased"] = stage.tile([P, 2, count, D], F32, tag="biased", name="biased")
-                live["plain"] = stage.tile([P, 2, count, D], F32, tag="plain", name="plain")
-            live["biased", i] = live["biased"]
-            live["plain", i] = live["plain"]
+        def staged(kind, i):
+            first, count = block_of[kind, i]
+            if (kind, first) not in live:
+                live[kind, first] = stage.tile([P, 2, count, D], F32, tag=kind, name=kind)
+            return live[kind, first], i - first
+
+        def send(kind, i, halves=(0, 1)):
+            first, count = block_of[kind, i]
+            if i == first + count - 1:
+                for half in halves:
+                    out = out_rows[half if kind == "biased" else 2 + half]
+                    block = live[kind, first][:, half, :, :]
+                    if count == 1:
+                        nc.sync.dma_start(out=out[:, first // GROUP, first % GROUP, :], in_=block[:, 0, :])
+                    else:
+                        nc.sync.dma_start(out=out[:, first // GROUP, :, :], in_=block)
 
         def add_biases(g, r):
             i = tiles_of(g)[0] + r
-            open_stage(i)
+            block, place = staged("biased", i)
             nc.vector.tensor_tensor(
-                out=live["biased", i][:, :, i - block_of[i][0], :],
+                out=block[:, :, place, :],
                 in0=live["q_biased", g, r][:].unsqueeze(1).to_broadcast([P, 2, D]),
                 in1=biases[:],
                 op=ALU.add,
             )
 
         def copy_out(g, r, wanted=(0, 1)):
-            i = tiles_of(g)[0] + r
-            open_stage(i)
-            for place in wanted:
-                acc = live[("q_plain", "v_plain")[place], g, r]
-                nc.scalar.copy(out=live["plain", i][:, place, i - block_of[i][0], :], in_=acc[:])
+            block, place = staged("plain", tiles_of(g)[0] + r)
+            for half in wanted:
+                acc = live[("q_plain", "v_plain")[half], g, r]
+                nc.scalar.copy(out=block[:, half, place, :], in_=acc[:])
 
         def store(g, r):
-            first, count = block_of[tiles_of(g)[0] + r]
-            if tiles_of(g)[0] + r == first + count - 1:
-                tiles = slice(first, first + count)
-                nc.sync.dma_start(out=out_rows[0][:, tiles, :], in_=live["biased", first][:, 0, :, :])
-                nc.sync.dma_start(out=out_rows[1][:, tiles, :], in_=live["biased", first][:, 1, :, :])
-                nc.sync.dma_start(out=out_rows[2][:, tiles, :], in_=live["plain", first][:, 0, :, :])
-                nc.sync.dma_start(out=out_rows[3][:, tiles, :], in_=live["plain", first][:, 1, :, :])
+            i = tiles_of(g)[0] + r
+            send("biased", i)
+            send("plain", i)
 
         row_statistics(0, 0)
         mean_and_rstd(0)
@@ -343,11 +359,15 @@ def tile_multiheadattentiowithrpe_pa_t_kernel(
         project(1, Q_PASSES)
         mean_and_rstd(3)
         add_biases(0, 0)
+        send("biased", 0)
         copy_out(0, 0, (0,))
+        send("plain", 0, (0,))
         scale_shift(2)
         quantise_weight(1)
         add_biases(1, 0)
+        send("biased", 1)
         copy_out(1, 0, (0,))
+        send("plain", 1, (0,))
         project(0, V_PASSES)
         project(1, V_PASSES)
         pack(2)
@@ -355,9 +375,9 @@ def tile_multiheadattentiowithrpe_pa_t_kernel(
         normalise(3)
         turn(3)
         copy_out(0, 0, (1,))
-        store(0, 0)
+        send("plain", 0, (1,))
         copy_out(1, 0, (1,))
-        store(1, 0)
+        send("plain", 1, (1,))
         row_statistics(4, 1)
         mean_and_rstd(4)
         for a in range(5, GROUPS + 3):

@@ -15,6 +15,7 @@ PACK = 4
 ROWS = 1024 * 4
 ROW_TILES = ROWS // P
 GROUP = 2
+ACT_FROM = 4
 HEAD = 2
 SINGLES_BIASED = 8
 SINGLES_PLAIN = 8
@@ -34,9 +35,9 @@ def tile_multiheadattentiowithrpe_pa_t_kernel(
     tc, x, gamma, beta, Wq, Wv, u_bias, v_bias, out_0, out_1, out_2, out_3
 ):
     nc = tc.nc
-    x_rows = x.rearrange("(j i) (c r) d -> (i c) j r d", i=P // 2, c=2)
+    x_rows = x.rearrange("(p a) b d -> p (a b) d", p=P)
     out_rows = [
-        o.rearrange("(j i) (c r) h f -> (i c) j r (h f)", i=P // 2, c=2) for o in (out_0, out_1, out_2, out_3)
+        o.rearrange("(p a) b h f -> p (a b) (h f)", p=P) for o in (out_0, out_1, out_2, out_3)
     ]
 
     with (
@@ -51,14 +52,7 @@ def tile_multiheadattentiowithrpe_pa_t_kernel(
 
         def load_rows(first, count):
             chunk = keep.tile([P, count, D], BF16, name="x_sb%d" % first)
-            pair = first // GROUP
-            if count == 1:
-                nc.sync.dma_start(out=chunk[:, 0, :], in_=x_rows[:, pair, first % GROUP, :])
-            else:
-                nc.sync.dma_start(
-                    out=chunk[:].rearrange("p (j r) d -> p j r d", r=GROUP),
-                    in_=x_rows[:, pair : pair + count // GROUP, :, :],
-                )
+            nc.sync.dma_start(out=chunk[:], in_=x_rows[:, first : first + count, :])
             for i in range(count):
                 x_home[first + i] = (chunk, i)
 
@@ -294,16 +288,12 @@ def tile_multiheadattentiowithrpe_pa_t_kernel(
                 live[kind, first] = stage.tile([P, 2, count, D], F32, tag=kind, name=kind)
             return live[kind, first], i - first
 
-        def send(kind, i, halves=(0, 1)):
+        def send(kind, i, halves=(0, 1), queue=nc.sync):
             first, count = block_of[kind, i]
             if i == first + count - 1:
                 for half in halves:
                     out = out_rows[half if kind == "biased" else 2 + half]
-                    block = live[kind, first][:, half, :, :]
-                    if count == 1:
-                        nc.sync.dma_start(out=out[:, first // GROUP, first % GROUP, :], in_=block[:, 0, :])
-                    else:
-                        nc.sync.dma_start(out=out[:, first // GROUP, :, :], in_=block)
+                    queue.dma_start(out=out[:, first : first + count, :], in_=live[kind, first][:, half, :, :])
 
         def add_biases(g, r):
             i = tiles_of(g)[0] + r
@@ -380,13 +370,16 @@ def tile_multiheadattentiowithrpe_pa_t_kernel(
         send("plain", 1, (1,))
         row_statistics(4, 1)
         mean_and_rstd(4)
-        for a in range(5, GROUPS + 3):
+        for a in range(5, GROUPS + 4):
             if a - 3 < GROUPS:
                 quantise(a - 3)
             if a - 3 < GROUPS:
                 project(a - 3, Q_PASSES + V_PASSES)
             if a - 2 < GROUPS:
                 scale_shift(a - 2)
+            if a - 4 >= ACT_FROM:
+                for r in range(tiles_of(a - 4)[1]):
+                    send("plain", tiles_of(a - 4)[0] + r, queue=nc.scalar)
             if a - 2 < GROUPS:
                 pack(a - 2)
             if a < GROUPS:
@@ -404,11 +397,15 @@ def tile_multiheadattentiowithrpe_pa_t_kernel(
                 mean_and_rstd(a)
             if a - 3 < GROUPS:
                 copy_out(a - 3, 0)
-                store(a - 3, 0)
+                send("biased", tiles_of(a - 3)[0] + 0)
+                if a - 3 < ACT_FROM:
+                    send("plain", tiles_of(a - 3)[0] + 0)
             if a - 3 < GROUPS:
                 if tiles_of(a - 3)[1] > 1:
                     add_biases(a - 3, 1)
             if a - 3 < GROUPS:
                 if tiles_of(a - 3)[1] > 1:
                     copy_out(a - 3, 1)
-                    store(a - 3, 1)
+                    send("biased", tiles_of(a - 3)[0] + 1)
+                    if a - 3 < ACT_FROM:
+                        send("plain", tiles_of(a - 3)[0] + 1)

@@ -379,7 +379,7 @@ def tile_multiheadattentiowithrpe_pa_t_kernel(
                 scale_shift(a - 2)
             if a - 4 >= ACT_FROM:
                 for r in range(tiles_of(a - 4)[1]):
-                    send("plain", tiles_of(a - 4)[0] + r, queue=nc.scalar)
+                    send("plain", tiles_of(a - 4)[0] + r, (1,), queue=nc.scalar)
             if a - 2 < GROUPS:
                 pack(a - 2)
             if a < GROUPS:
@@ -398,8 +398,7 @@ def tile_multiheadattentiowithrpe_pa_t_kernel(
             if a - 3 < GROUPS:
                 copy_out(a - 3, 0)
                 send("biased", tiles_of(a - 3)[0] + 0)
-                if a - 3 < ACT_FROM:
-                    send("plain", tiles_of(a - 3)[0] + 0)
+                send("plain", tiles_of(a - 3)[0] + 0, (0, 1) if a - 3 < ACT_FROM else (0,))
             if a - 3 < GROUPS:
                 if tiles_of(a - 3)[1] > 1:
                     add_biases(a - 3, 1)
@@ -407,5 +406,4 @@ def tile_multiheadattentiowithrpe_pa_t_kernel(
                 if tiles_of(a - 3)[1] > 1:
                     copy_out(a - 3, 1)
                     send("biased", tiles_of(a - 3)[0] + 1)
-                    if a - 3 < ACT_FROM:
-                        send("plain", tiles_of(a - 3)[0] + 1)
+                    send("plain", tiles_of(a - 3)[0] + 1, (0, 1) if a - 3 < ACT_FROM else (0,))

import concourse.mybir as mybir
from concourse.masks import make_identity

F32 = mybir.dt.float32
BF16 = mybir.dt.bfloat16
U32 = mybir.dt.uint32
U8 = mybir.dt.uint8
FP8X4 = mybir.dt.float8_e4m3fn_x4
ACT = mybir.ActivationFunctionType
ALU = mybir.AluOpType

P = 128
D = 512
PACK = 4
ROWS = 1024 * 4
ROW_TILES = ROWS // P
GROUP = 2
ACT_FROM = 4
HEAD = 2
SINGLES_BIASED = 8
SINGLES_PLAIN = 8
TAIL = 0
PAIRS = (ROW_TILES - HEAD - TAIL) // GROUP
GROUPS = HEAD + PAIRS + TAIL
BANK = 512
LOAD_TILES = 4
GPSIMD_EVERY = 2
RUN = 4
EPS = 1e-5

FLOPS = 2 * ROWS * D * (2 * D)


def tile_multiheadattentiowithrpe_pa_t_kernel(
    tc, x, gamma, beta, Wq, Wv, u_bias, v_bias, out_0, out_1, out_2, out_3
):
    nc = tc.nc
    x_rows = x.rearrange("(p a) b d -> p (a b) d", p=P)
    out_rows = [
        o.rearrange("(p a) b h f -> p (a b) (h f)", p=P) for o in (out_0, out_1, out_2, out_3)
    ]

    with (
        tc.tile_pool(name="keep", bufs=1) as keep,
        tc.tile_pool(name="small", bufs=4) as small,
        tc.tile_pool(name="work", bufs=2) as work,
        tc.tile_pool(name="stage", bufs=4) as stage,
        tc.psum_pool(name="psum", bufs=2) as psum,
        tc.manual_schedule(),
    ):
        x_home = {}

        def load_rows(first, count):
            chunk = keep.tile([P, count, D], BF16, name="x_sb%d" % first)
            nc.sync.dma_start(out=chunk[:], in_=x_rows[:, first : first + count, :])
            for i in range(count):
                x_home[first + i] = (chunk, i)

        def load_weight(weight, name):
            raw = keep.tile([P, PACK, D], BF16, name=name)
            nc.sync.dma_start(out=raw[:], in_=weight.rearrange("(p t) n -> p t n", t=PACK))
            return raw

        load_rows(0, 1)
        load_rows(1, 1)
        load_rows(2, 2)
        wq_raw = load_weight(Wq, "wq_raw")
        wv_raw = load_weight(Wv, "wv_raw")
        for first in range(4, ROW_TILES, LOAD_TILES):
            load_rows(first, LOAD_TILES)
        w_raw = [wq_raw, wv_raw]

        vec_rows = keep.tile([P, D], BF16, name="vec_rows")
        nc.vector.memset(vec_rows[:], 0.0)
        minus_half = keep.tile([P, GROUP, 1], F32, name="minus_half")
        nc.vector.memset(minus_half[:], -0.5)
        stats = keep.tile([P, ROW_TILES, 9], F32, name="stats")
        nc.gpsimd.memset(stats[:, :, 6:8], 0.0)
        nc.gpsimd.memset(stats[:, :, 8:9], D * EPS)
        minus_one = keep.tile([P, 1], F32, name="minus_one")
        nc.vector.memset(minus_one[:], -1.0)
        nc.scalar.dma_start(out=vec_rows[0:1, :], in_=gamma.unsqueeze(0))
        nc.scalar.dma_start(out=vec_rows[1:2, :], in_=beta.unsqueeze(0))
        nc.scalar.dma_start(out=vec_rows[2:3, :], in_=u_bias.rearrange("h f -> (h f)").unsqueeze(0))
        nc.scalar.dma_start(out=vec_rows[3:4, :], in_=v_bias.rearrange("h f -> (h f)").unsqueeze(0))
        ident = keep.tile([P, P], F32, name="ident")
        make_identity(nc, ident[:])
        ident_bf = keep.tile([P, P], BF16, name="ident_bf")
        nc.vector.tensor_copy(out=ident_bf[:], in_=ident[:])
        warm = keep.tile([P, 1], F32, name="warm")
        nc.scalar.activation(out=warm[:], in_=minus_half[:, 0, :], func=ACT.Identity)
        gain_offset = keep.tile([P, PACK, 2], F32, name="gain_offset")
        biases = keep.tile([P, 2, D], F32, name="biases")
        w_grouped = [
            keep.tile([P, D, PACK], BF16, name="w_grouped%d" % w, align_bytes=64) for w in range(2)
        ]
        w_codes = keep.tile([P, 2, D], U32, name="w_codes", align_bytes=64)
        w_scales = keep.tile([P, 2, D], U8, name="w_scales", align_bytes=64)

        def turn_gamma_beta():
            vec_cols = psum.tile([P, PACK, P], BF16, tag="turned", name="vec_cols")
            for t in range(PACK):
                nc.tensor.transpose(
                    vec_cols[:, t, :], vec_rows[:].rearrange("p (m t) -> p t m", t=PACK)[:, t, :], ident_bf[:]
                )
            live["vec_cols"] = vec_cols

        def take_gain():
            nc.scalar.copy(out=gain_offset[:], in_=live["vec_cols"][:, :, 0:2])

        def group_weight(w, copy, part=0, parts=1):
            cols = slice(part * D // parts, (part + 1) * D // parts)
            copy(
                out=w_grouped[w][:, cols, :].rearrange("p (c i) t -> p c t i", i=RUN),
                in_=w_raw[w][:, :, cols].rearrange("p t (c i) -> p c t i", i=RUN),
            )

        def gp_copy(out, in_):
            nc.gpsimd.tensor_scalar(out=out, in0=in_, scalar1=1.0, scalar2=0.0, op0=ALU.mult, op1=ALU.add)

        def quantise_weight(w):
            nc.vector.quantize_mx(
                out=w_codes[:, w, :].bitcast(FP8X4),
                scales=w_scales[:, w, :],
                in_=w_grouped[w][:].rearrange("p c t -> p (c t)"),
            )

        def spread_bias(b):
            bias_ps = psum.tile([P, D], F32, tag=("q_plain", "v_plain")[b], name="bias_ps")
            nc.tensor.matmul(
                out=bias_ps[:], lhsT=ident_bf[:, 2 + b : 3 + b].to_broadcast([P, P]), rhs=vec_rows[:],
                start=True, stop=True,
            )
            nc.scalar.copy(out=biases[:, b, :], in_=bias_ps[:])

        def tiles_of(g):
            if g < HEAD:
                return g, 1
            if g < HEAD + PAIRS:
                return HEAD + (g - HEAD) * GROUP, GROUP
            return ROW_TILES - GROUPS + g, 1

        def rows_of(g):
            first, count = tiles_of(g)
            homes = [x_home[first + r] for r in range(count)]
            return [chunk[:, i, :] for chunk, i in homes]

        live = {}

        def row_statistics(g, r):
            nc.vector.bn_stats(out=stats[:, tiles_of(g)[0] + r, 0:6], in_=rows_of(g)[r])

        def norm_engine(g, r):
            return "V" if g < HEAD or r == 1 else "S"

        def mean_and_rstd(g):
            first, count = tiles_of(g)
            mean_var = small.tile([P, GROUP, 2], F32, tag="mean_var", name="mean_var")
            for r in range(count):
                nc.vector.bn_aggr(out=mean_var[:, r, :], in_=stats[:, first + r, :])
            rstd = small.tile([P, GROUP, 1], F32, tag="rstd", name="rstd")
            nc.gpsimd.tensor_tensor(
                out=rstd[:, :count], in0=mean_var[:, :count, 1:2], in1=minus_half[:, :count], op=ALU.pow
            )
            live["mean_var", g] = mean_var
            live["rstd", g] = rstd
            if all(norm_engine(g, r) == "V" for r in range(count)):
                return
            shift = small.tile([P, GROUP, 1], F32, tag="shift", name="shift")
            for r in range(count):
                if norm_engine(g, r) == "V":
                    continue
                nc.gpsimd.tensor_scalar(
                    out=shift[:, r, :], in0=mean_var[:, r, 0:1], scalar1=rstd[:, r, :], scalar2=minus_one[:],
                    op0=ALU.mult, op1=ALU.mult,
                )
            live["shift", g] = shift

        def normalise(g):
            normal = work.tile([P, GROUP, D], F32, tag="normal", name="normal")
            for r, rows in enumerate(rows_of(g)):
                by_m = rows.rearrange("p (m t) -> p t m", t=PACK)
                by_t = normal[:, r, :].rearrange("p (t m) -> p t m", t=PACK)
                rstd = live["rstd", g][:, r, :]
                if norm_engine(g, r) == "V":
                    nc.vector.tensor_scalar(
                        out=by_t, in0=by_m, scalar1=live["mean_var", g][:, r, 0:1], scalar2=rstd,
                        op0=ALU.subtract, op1=ALU.mult,
                    )
                    continue
                shift = live["shift", g][:, r, :]
                if norm_engine(g, r) == "G":
                    nc.gpsimd.tensor_scalar(
                        out=by_t, in0=by_m, scalar1=rstd, scalar2=shift, op0=ALU.mult, op1=ALU.add
                    )
                else:
                    nc.scalar.activation(out=by_t, in_=by_m, func=ACT.Identity, scale=rstd, bias=shift)
            live["normal", g] = normal

        def turn(g):
            count = tiles_of(g)[1]
            per_bank = BANK // (count * P)
            banks = [
                psum.tile([P, per_bank, count, P], F32, tag="turned", name="turned%d" % b)
                for b in range(PACK // per_bank)
            ]
            chunks = [banks[t // per_bank][:, t % per_bank, :, :] for t in range(PACK)]
            for r in range(count):
                for t in range(PACK):
                    nc.tensor.transpose(
                        chunks[t][:, r, :], live["normal", g][:, r, t * P : (t + 1) * P], ident[:]
                    )
            live["turned", g] = chunks

        def scale_shift(g):
            columns = tiles_of(g)[1] * P
            planes = work.tile([P, PACK, columns], BF16, tag="planes", name="planes")
            for t in range(PACK):
                nc.scalar.activation(
                    out=planes[:, t, :],
                    in_=live["turned", g][t].rearrange("p r c -> p (r c)"),
                    func=ACT.Identity,
                    scale=gain_offset[:, t, 0:1],
                    bias=gain_offset[:, t, 1:2],
                )
            live["planes", g] = planes

        def pack_on_gpsimd(g):
            return g > HEAD

        def pack(g):
            columns = tiles_of(g)[1] * P
            grouped = work.tile([P, columns, PACK], BF16, tag="grouped", name="grouped", align_bytes=64)
            by_row = grouped[:].rearrange("p (c i) t -> p c t i", i=RUN)
            by_plane = live["planes", g][:].rearrange("p t (c i) -> p c t i", i=RUN)
            if pack_on_gpsimd(g):
                nc.gpsimd.tensor_scalar(
                    out=by_row, in0=by_plane, scalar1=1.0, scalar2=0.0, op0=ALU.mult, op1=ALU.add
                )
            else:
                nc.vector.tensor_copy(out=by_row, in_=by_plane)
            live["grouped", g] = grouped

        def quantise(g):
            columns = tiles_of(g)[1] * P
            codes = work.tile([P, columns], U32, tag="codes", name="codes", align_bytes=64)
            scales = work.tile([P, columns], U8, tag="scales", name="scales", align_bytes=64)
            nc.vector.quantize_mx(
                out=codes[:].bitcast(FP8X4),
                scales=scales[:],
                in_=live["grouped", g][:].rearrange("p c t -> p (c t)"),
            )
            live["codes", g] = codes
            live["scales", g] = scales

        def project(g, wanted):
            for r in range(tiles_of(g)[1]):
                cols = slice(r * P, (r + 1) * P)
                for tag, w in wanted:
                    acc = psum.tile([P, D], F32, tag=tag, name=tag)
                    nc.tensor.matmul_mx(
                        out=acc[:],
                        lhsT=live["codes", g][:, cols].bitcast(FP8X4),
                        lhsT_scale=live["scales", g][:, cols],
                        rhs=w_codes[:, w, :].bitcast(FP8X4),
                        rhs_scale=w_scales[:, w, :],
                        start=True,
                        stop=True,
                    )
                    live[tag, g, r] = acc

        Q_PASSES = (("q_biased", 0), ("q_plain", 0))
        V_PASSES = (("v_plain", 1),)

        block_of = {}
        for kind, singles in (("biased", SINGLES_BIASED), ("plain", SINGLES_PLAIN)):
            first = 0
            lengths = [1] * singles + [GROUP] * ROW_TILES
            while first < ROW_TILES:
                count = min(lengths.pop(0), ROW_TILES - first)
                for i in range(first, first + count):
                    block_of[kind, i] = (first, count)
                first += count

        def staged(kind, i):
            first, count = block_of[kind, i]
            if (kind, first) not in live:
                live[kind, first] = stage.tile([P, 2, count, D], F32, tag=kind, name=kind)
            return live[kind, first], i - first

        def send(kind, i, halves=(0, 1), queue=nc.sync):
            first, count = block_of[kind, i]
            if i == first + count - 1:
                for half in halves:
                    out = out_rows[half if kind == "biased" else 2 + half]
                    queue.dma_start(out=out[:, first : first + count, :], in_=live[kind, first][:, half, :, :])

        def add_biases(g, r):
            i = tiles_of(g)[0] + r
            block, place = staged("biased", i)
            nc.vector.tensor_tensor(
                out=block[:, :, place, :],
                in0=live["q_biased", g, r][:].unsqueeze(1).to_broadcast([P, 2, D]),
                in1=biases[:],
                op=ALU.add,
            )

        def copy_out(g, r, wanted=(0, 1)):
            block, place = staged("plain", tiles_of(g)[0] + r)
            for half in wanted:
                acc = live[("q_plain", "v_plain")[half], g, r]
                nc.scalar.copy(out=block[:, half, place, :], in_=acc[:])

        def store(g, r):
            i = tiles_of(g)[0] + r
            send("biased", i)
            send("plain", i)

        row_statistics(0, 0)
        mean_and_rstd(0)
        row_statistics(1, 0)
        mean_and_rstd(1)
        turn_gamma_beta()
        take_gain()
        spread_bias(0)
        spread_bias(1)
        normalise(0)
        turn(0)
        row_statistics(2, 0)
        row_statistics(2, 1)
        group_weight(0, nc.vector.tensor_copy)
        scale_shift(0)
        mean_and_rstd(2)
        normalise(1)
        turn(1)
        quantise_weight(0)
        pack(0)
        group_weight(1, nc.scalar.copy, 0, 2)
        scale_shift(1)
        row_statistics(3, 0)
        quantise(0)
        project(0, Q_PASSES)
        pack(1)
        row_statistics(3, 1)
        normalise(2)
        turn(2)
        group_weight(1, nc.scalar.copy, 1, 2)
        quantise(1)
        project(1, Q_PASSES)
        mean_and_rstd(3)
        add_biases(0, 0)
        send("biased", 0)
        copy_out(0, 0, (0,))
        send("plain", 0, (0,))
        scale_shift(2)
        quantise_weight(1)
        add_biases(1, 0)
        send("biased", 1)
        copy_out(1, 0, (0,))
        send("plain", 1, (0,))
        project(0, V_PASSES)
        project(1, V_PASSES)
        pack(2)
        row_statistics(4, 0)
        normalise(3)
        turn(3)
        copy_out(0, 0, (1,))
        send("plain", 0, (1,))
        copy_out(1, 0, (1,))
        send("plain", 1, (1,))
        row_statistics(4, 1)
        mean_and_rstd(4)
        for a in range(5, GROUPS + 4):
            if a - 3 < GROUPS:
                quantise(a - 3)
            if a - 3 < GROUPS:
                project(a - 3, Q_PASSES + V_PASSES)
            if a - 2 < GROUPS:
                scale_shift(a - 2)
            if a - 4 >= ACT_FROM:
                for r in range(tiles_of(a - 4)[1]):
                    send("plain", tiles_of(a - 4)[0] + r, (1,), queue=nc.scalar)
            if a - 2 < GROUPS:
                pack(a - 2)
            if a < GROUPS:
                row_statistics(a, 0)
            if a - 3 < GROUPS:
                add_biases(a - 3, 0)
            if a < GROUPS:
                if tiles_of(a)[1] > 1:
                    row_statistics(a, 1)
            if a - 1 < GROUPS:
                normalise(a - 1)
            if a - 1 < GROUPS:
                turn(a - 1)
            if a < GROUPS:
                mean_and_rstd(a)
            if a - 3 < GROUPS:
                copy_out(a - 3, 0)
                send("biased", tiles_of(a - 3)[0] + 0)
                send("plain", tiles_of(a - 3)[0] + 0, (0, 1) if a - 3 < ACT_FROM else (0,))
            if a - 3 < GROUPS:
                if tiles_of(a - 3)[1] > 1:
                    add_biases(a - 3, 1)
            if a - 3 < GROUPS:
                if tiles_of(a - 3)[1] > 1:
                    copy_out(a - 3, 1)
                    send("biased", tiles_of(a - 3)[0] + 1)
                    send("plain", tiles_of(a - 3)[0] + 1, (0, 1) if a - 3 < ACT_FROM else (0,))
